import numpy as np
import ml_dtypes

BF16 = ml_dtypes.bfloat16


def bf(x):
    return np.asarray(x, np.float32).astype(BF16)


def f32(x):
    return np.asarray(x, np.float32)


def f64(x):
    return np.asarray(x).astype(np.float64)


def striped(idx):
    return np.tile(idx.reshape(-1, 16).T, (8, 1))


C, S, E, K, P, N, T = 512, 2048, 16, 3, 1, 256, 9


def setup_inputs():
    return {"base": f32(np.random.standard_normal((C, S))), "x": f32(np.random.standard_normal((1, E, E))), "wts": f32(np.random.random((C, T, N))), "offs": striped(np.random.permutation(S)[:N])}


def reference(base, x, wts, offs):
    idx = offs[:16].T.reshape(-1)
    px = np.pad(f64(x)[0], P)
    w = f64(wts).reshape(C, K, K, E, E)
    acc = np.zeros((C, E, E))
    for i in range(K):
        for j in range(K):
            acc = acc + w[:, i, j] * px[None, i:i + E, j:j + E]
    out = f64(base).copy()
    out[:, idx] = acc.reshape(C, N)
    return out

@@ -1,0 +1,63 @@
+import concourse.mybir as mybir
+
+F32 = mybir.dt.float32
+U16 = mybir.dt.uint16
+MULT = mybir.AluOpType.mult
+ADD = mybir.AluOpType.add
+
+P = 128
+C, S = 512, 2048
+E, K = 16, 3
+N = E * E
+BLOCKS = C // P
+FLOPS = 2 * C * K * K * N
+
+
+def tile_locallyconnected2d_kernel(tc, base, x, wts, offs, out):
+    nc = tc.nc
+    with (
+        tc.tile_pool(name="held", bufs=1) as held,
+        tc.tile_pool(name="windows", bufs=BLOCKS) as windows,
+        tc.tile_pool(name="weights", bufs=BLOCKS * K) as weights,
+        tc.tile_pool(name="work", bufs=4) as work,
+    ):
+        offsets = held.tile([P, N // 16], U16, name="offsets")
+        nc.sync.dma_start(offsets[:], offs)
+
+        image = held.tile([P, N], F32, name="image")
+        nc.scalar.dma_start(image[:], x.rearrange("o h w -> (o h w)").partition_broadcast(P))
+
+        shifted = held.tile([P, K, (E + 2) * E], F32, name="shifted")
+        nc.vector.memset(shifted[:], 0.0)
+        shifted_rows = shifted[:].rearrange("p j (a q) -> p j a q", q=E)
+        image_rows = image[:].rearrange("p (h w) -> p h w", w=E)
+        for j in range(K):
+            first, last = max(0, 1 - j), min(E, E + 1 - j)
+            nc.vector.tensor_copy(
+                shifted_rows[:, j, 1 : E + 1, first:last],
+                image_rows[:, :, first + j - 1 : last + j - 1],
+            )
+
+        for b in range(BLOCKS):
+            channels = slice(b * P, (b + 1) * P)
+
+            rows = None
+            for i in range(K):
+                w = weights.tile([P, K, N], F32, name="w")
+                nc.sync.dma_start(w[:], wts[channels, i * K : (i + 1) * K, :])
+                prod = work.tile([P, K, N], F32, name="prod")
+                nc.vector.tensor_tensor(prod[:], w[:], shifted[:, :, i * E : i * E + N], MULT)
+                if i == 0:
+                    rows = prod
+                else:
+                    more = work.tile([P, K, N], F32, name="more")
+                    nc.vector.tensor_tensor(more[:], rows[:], prod[:], ADD)
+                    rows = more
+
+            window = windows.tile([P, S], F32, name="window")
+            nc.sync.dma_start(window[:], base[channels, :])
+
+            pair = work.tile([P, N], F32, name="pair")
+            nc.vector.tensor_tensor(pair[:], rows[:, 0, :], rows[:, 1, :], ADD)
+            nc.vector.tensor_tensor(window[:].indirect(offsets[:]), pair[:], rows[:, 2, :], ADD)
+            nc.scalar.dma_start(out[channels, :], window[:])

@@ -1,4 +1,5 @@
 import concourse.mybir as mybir
+from concourse.masks import make_identity
 
 F32 = mybir.dt.float32
 U16 = mybir.dt.uint16
@@ -9,9 +10,9 @@ P = 128
 C, S = 512, 2048
 E, K = 16, 3
 N = E * E
+T = K * K
 BLOCKS = C // P
-FLOPS = 2 * C * K * K * N
-
+FLOPS = 2 * C * T * N
 
 def tile_locallyconnected2d_kernel(tc, base, x, wts, offs, out):
     nc = tc.nc
@@ -20,12 +21,27 @@ def tile_locallyconnected2d_kernel(tc, base, x, wts, offs, out):
         tc.tile_pool(name="windows", bufs=BLOCKS) as windows,
         tc.tile_pool(name="weights", bufs=BLOCKS * K) as weights,
         tc.tile_pool(name="work", bufs=4) as work,
+        tc.psum_pool(name="psum", bufs=2) as psum,
     ):
         offsets = held.tile([P, N // 16], U16, name="offsets")
         nc.sync.dma_start(offsets[:], offs)
 
         image = held.tile([P, N], F32, name="image")
         nc.scalar.dma_start(image[:], x.rearrange("o h w -> (o h w)").partition_broadcast(P))
+
+        all_w, all_windows = [], []
+        for b in range(BLOCKS):
+            channels = slice(b * P, (b + 1) * P)
+            for i in range(K):
+                w = weights.tile([P, K, N], F32, name="w")
+                nc.sync.dma_start(w[:], wts[channels, i * K : (i + 1) * K, :])
+                all_w.append(w)
+            window = windows.tile([P, S], F32, name="window")
+            nc.sync.dma_start(window[:], base[channels, :])
+            all_windows.append(window)
+
+        identity = held.tile([P, P], F32, name="identity")
+        make_identity(nc, identity[:])
 
         shifted = held.tile([P, K, (E + 2) * E], F32, name="shifted")
         nc.vector.memset(shifted[:], 0.0)
@@ -38,26 +54,24 @@ def tile_locallyconnected2d_kernel(tc, base, x, wts, offs, out):
                 image_rows[:, :, first + j - 1 : last + j - 1],
             )
 
+        def place(b, acc, prod):
+            most = work.tile([P, N], F32, name="most")
+            nc.vector.tensor_tensor(most[:], acc[:], prod[:, 1, :], ADD)
+            window = all_windows[b]
+            nc.vector.tensor_tensor(window[:].indirect(offsets[:]), most[:], prod[:, 2, :], ADD)
+            nc.sync.dma_start(out[b * P : (b + 1) * P, :], window[:])
+
+        waiting = None
         for b in range(BLOCKS):
-            channels = slice(b * P, (b + 1) * P)
-
-            rows = None
+            acc = psum.tile([P, N], F32, name="acc")
             for i in range(K):
-                w = weights.tile([P, K, N], F32, name="w")
-                nc.sync.dma_start(w[:], wts[channels, i * K : (i + 1) * K, :])
                 prod = work.tile([P, K, N], F32, name="prod")
-                nc.vector.tensor_tensor(prod[:], w[:], shifted[:, :, i * E : i * E + N], MULT)
-                if i == 0:
-                    rows = prod
-                else:
-                    more = work.tile([P, K, N], F32, name="more")
-                    nc.vector.tensor_tensor(more[:], rows[:], prod[:], ADD)
-                    rows = more
-
-            window = windows.tile([P, S], F32, name="window")
-            nc.sync.dma_start(window[:], base[channels, :])
-
-            pair = work.tile([P, N], F32, name="pair")
-            nc.vector.tensor_tensor(pair[:], rows[:, 0, :], rows[:, 1, :], ADD)
-            nc.vector.tensor_tensor(window[:].indirect(offsets[:]), pair[:], rows[:, 2, :], ADD)
-            nc.scalar.dma_start(out[channels, :], window[:])
+                nc.vector.tensor_tensor(prod[:], all_w[b * K + i][:], shifted[:, :, i * E : i * E + N], MULT)
+                for j in range(K):
+                    t = i * K + j
+                    if t <= T - 3:
+                        nc.tensor.matmul(acc[:], identity[:], prod[:, j, :], start=(t == 0), stop=(t == T - 3))
+                if i == 0 and waiting is not None:
+                    place(*waiting)
+            waiting = (b, acc, prod)
+        place(*waiting)

@@ -13,14 +13,15 @@ N = E * E
 T = K * K
 BLOCKS = C // P
 FLOPS = 2 * C * T * N
+LAG = 1
 
 def tile_locallyconnected2d_kernel(tc, base, x, wts, offs, out):
     nc = tc.nc
     with (
         tc.tile_pool(name="held", bufs=1) as held,
         tc.tile_pool(name="windows", bufs=BLOCKS) as windows,
-        tc.tile_pool(name="weights", bufs=BLOCKS * K) as weights,
-        tc.tile_pool(name="work", bufs=4) as work,
+        tc.tile_pool(name="weights", bufs=BLOCKS) as weights,
+        tc.tile_pool(name="work", bufs=6) as work,
         tc.psum_pool(name="psum", bufs=2) as psum,
     ):
         offsets = held.tile([P, N // 16], U16, name="offsets")
@@ -30,15 +31,17 @@ def tile_locallyconnected2d_kernel(tc, base, x, wts, offs, out):
         nc.scalar.dma_start(image[:], x.rearrange("o h w -> (o h w)").partition_broadcast(P))
 
         all_w, all_windows = [], []
-        for b in range(BLOCKS):
-            channels = slice(b * P, (b + 1) * P)
-            for i in range(K):
-                w = weights.tile([P, K, N], F32, name="w")
-                nc.sync.dma_start(w[:], wts[channels, i * K : (i + 1) * K, :])
+        for b in range(BLOCKS + 1):
+            if b < BLOCKS:
+                w = weights.tile([P, T, N], F32, name="w")
+                taps = K if b == 0 else T
+                for t in range(0, T, taps):
+                    nc.sync.dma_start(w[:, t : t + taps, :], wts[b * P : (b + 1) * P, t : t + taps, :])
                 all_w.append(w)
-            window = windows.tile([P, S], F32, name="window")
-            nc.sync.dma_start(window[:], base[channels, :])
-            all_windows.append(window)
+            if b > 0:
+                window = windows.tile([P, S], F32, name="window")
+                nc.sync.dma_start(window[:], base[(b - 1) * P : b * P, :])
+                all_windows.append(window)
 
         identity = held.tile([P, P], F32, name="identity")
         make_identity(nc, identity[:])
@@ -66,12 +69,12 @@ def tile_locallyconnected2d_kernel(tc, base, x, wts, offs, out):
             acc = psum.tile([P, N], F32, name="acc")
             for i in range(K):
                 prod = work.tile([P, K, N], F32, name="prod")
-                nc.vector.tensor_tensor(prod[:], all_w[b * K + i][:], shifted[:, :, i * E : i * E + N], MULT)
+                nc.vector.tensor_tensor(prod[:], all_w[b][:, i * K : (i + 1) * K, :], shifted[:, :, i * E : i * E + N], MULT)
                 for j in range(K):
                     t = i * K + j
                     if t <= T - 3:
                         nc.tensor.matmul(acc[:], identity[:], prod[:, j, :], start=(t == 0), stop=(t == T - 3))
-                if i == 0 and waiting is not None:
+                if i == LAG and waiting is not None:
                     place(*waiting)
             waiting = (b, acc, prod)
         place(*waiting)

@@ -12,8 +12,9 @@ E, K = 16, 3
 N = E * E
 T = K * K
 BLOCKS = C // P
+ON_TENSOR = T - 2
 FLOPS = 2 * C * T * N
-LAG = 1
+
 
 def tile_locallyconnected2d_kernel(tc, base, x, wts, offs, out):
     nc = tc.nc
@@ -21,7 +22,7 @@ def tile_locallyconnected2d_kernel(tc, base, x, wts, offs, out):
         tc.tile_pool(name="held", bufs=1) as held,
         tc.tile_pool(name="windows", bufs=BLOCKS) as windows,
         tc.tile_pool(name="weights", bufs=BLOCKS) as weights,
-        tc.tile_pool(name="work", bufs=6) as work,
+        tc.tile_pool(name="work", bufs=2 * K) as work,
         tc.psum_pool(name="psum", bufs=2) as psum,
     ):
         offsets = held.tile([P, N // 16], U16, name="offsets")
@@ -57,24 +58,29 @@ def tile_locallyconnected2d_kernel(tc, base, x, wts, offs, out):
                 image_rows[:, :, first + j - 1 : last + j - 1],
             )
 
-        def place(b, acc, prod):
-            most = work.tile([P, N], F32, name="most")
-            nc.vector.tensor_tensor(most[:], acc[:], prod[:, 1, :], ADD)
-            window = all_windows[b]
-            nc.vector.tensor_tensor(window[:].indirect(offsets[:]), most[:], prod[:, 2, :], ADD)
-            nc.sync.dma_start(out[b * P : (b + 1) * P, :], window[:])
-
-        waiting = None
-        for b in range(BLOCKS):
+        def multiply(b):
             acc = psum.tile([P, N], F32, name="acc")
             for i in range(K):
                 prod = work.tile([P, K, N], F32, name="prod")
-                nc.vector.tensor_tensor(prod[:], all_w[b][:, i * K : (i + 1) * K, :], shifted[:, :, i * E : i * E + N], MULT)
+                nc.vector.tensor_tensor(
+                    prod[:], all_w[b][:, i * K : (i + 1) * K, :], shifted[:, :, i * E : i * E + N], MULT
+                )
                 for j in range(K):
                     t = i * K + j
-                    if t <= T - 3:
-                        nc.tensor.matmul(acc[:], identity[:], prod[:, j, :], start=(t == 0), stop=(t == T - 3))
-                if i == LAG and waiting is not None:
-                    place(*waiting)
-            waiting = (b, acc, prod)
-        place(*waiting)
+                    if t < ON_TENSOR:
+                        nc.tensor.matmul(acc[:], identity[:], prod[:, j, :], start=(t == 0), stop=(t == ON_TENSOR - 1))
+            return acc, prod
+
+        def place(b, acc, prod):
+            most = work.tile([P, N], F32, name="most")
+            nc.vector.tensor_tensor(most[:], acc[:], prod[:, K - 2, :], ADD)
+            window = all_windows[b]
+            nc.vector.tensor_tensor(window[:].indirect(offsets[:]), most[:], prod[:, K - 1, :], ADD)
+            nc.sync.dma_start(out[b * P : (b + 1) * P, :], window[:])
+
+        parts = multiply(0)
+        for b in range(1, BLOCKS):
+            parts_ahead = multiply(b)
+            place(b - 1, *parts)
+            parts = parts_ahead
+        place(BLOCKS - 1, *parts)

@@ -12,9 +12,7 @@ E, K = 16, 3
 N = E * E
 T = K * K
 BLOCKS = C // P
-ON_TENSOR = T - 2
 FLOPS = 2 * C * T * N
-
 
 def tile_locallyconnected2d_kernel(tc, base, x, wts, offs, out):
     nc = tc.nc
@@ -62,25 +60,26 @@ def tile_locallyconnected2d_kernel(tc, base, x, wts, offs, out):
             acc = psum.tile([P, N], F32, name="acc")
             for i in range(K):
                 prod = work.tile([P, K, N], F32, name="prod")
-                nc.vector.tensor_tensor(
-                    prod[:], all_w[b][:, i * K : (i + 1) * K, :], shifted[:, :, i * E : i * E + N], MULT
-                )
-                for j in range(K):
-                    t = i * K + j
-                    if t < ON_TENSOR:
-                        nc.tensor.matmul(acc[:], identity[:], prod[:, j, :], start=(t == 0), stop=(t == ON_TENSOR - 1))
-            return acc, prod
+                nc.vector.tensor_tensor(prod[:], all_w[b][:, i * K : (i + 1) * K, :], shifted[:, :, i * E : i * E + N], MULT)
+                if i < K - 1:
+                    for j in range(K):
+                        nc.tensor.matmul(
+                            acc[:], identity[:], prod[:, j, :], start=(i == 0 and j == 0), stop=(i == K - 2 and j == K - 1)
+                        )
+            pair = work.tile([P, N], F32, name="pair")
+            nc.vector.tensor_tensor(pair[:], prod[:, 0, :], prod[:, 1, :], ADD)
+            return acc, pair, prod[:, 2, :]
 
-        def place(b, acc, prod):
+        def place(b, acc, pair, tap8):
             most = work.tile([P, N], F32, name="most")
-            nc.vector.tensor_tensor(most[:], acc[:], prod[:, K - 2, :], ADD)
+            nc.vector.tensor_tensor(most[:], acc[:], pair[:], ADD)
             window = all_windows[b]
-            nc.vector.tensor_tensor(window[:].indirect(offsets[:]), most[:], prod[:, K - 1, :], ADD)
+            nc.vector.tensor_tensor(window[:].indirect(offsets[:]), most[:], tap8, ADD)
             nc.sync.dma_start(out[b * P : (b + 1) * P, :], window[:])
 
         parts = multiply(0)
         for b in range(1, BLOCKS):
-            parts_ahead = multiply(b)
+            next_parts = multiply(b)
             place(b - 1, *parts)
-            parts = parts_ahead
+            parts = next_parts
         place(BLOCKS - 1, *parts)

@@ -12,7 +12,9 @@ E, K = 16, 3
 N = E * E
 T = K * K
 BLOCKS = C // P
+ON_TENSOR = T - 2
 FLOPS = 2 * C * T * N
+
 
 def tile_locallyconnected2d_kernel(tc, base, x, wts, offs, out):
     nc = tc.nc
@@ -33,9 +35,7 @@ def tile_locallyconnected2d_kernel(tc, base, x, wts, offs, out):
         for b in range(BLOCKS + 1):
             if b < BLOCKS:
                 w = weights.tile([P, T, N], F32, name="w")
-                taps = K if b == 0 else T
-                for t in range(0, T, taps):
-                    nc.sync.dma_start(w[:, t : t + taps, :], wts[b * P : (b + 1) * P, t : t + taps, :])
+                nc.sync.dma_start(w[:], wts[b * P : (b + 1) * P, :, :])
                 all_w.append(w)
             if b > 0:
                 window = windows.tile([P, S], F32, name="window")
@@ -60,26 +60,25 @@ def tile_locallyconnected2d_kernel(tc, base, x, wts, offs, out):
             acc = psum.tile([P, N], F32, name="acc")
             for i in range(K):
                 prod = work.tile([P, K, N], F32, name="prod")
-                nc.vector.tensor_tensor(prod[:], all_w[b][:, i * K : (i + 1) * K, :], shifted[:, :, i * E : i * E + N], MULT)
-                if i < K - 1:
-                    for j in range(K):
-                        nc.tensor.matmul(
-                            acc[:], identity[:], prod[:, j, :], start=(i == 0 and j == 0), stop=(i == K - 2 and j == K - 1)
-                        )
-            pair = work.tile([P, N], F32, name="pair")
-            nc.vector.tensor_tensor(pair[:], prod[:, 0, :], prod[:, 1, :], ADD)
-            return acc, pair, prod[:, 2, :]
+                nc.vector.tensor_tensor(
+                    prod[:], all_w[b][:, i * K : (i + 1) * K, :], shifted[:, :, i * E : i * E + N], MULT
+                )
+                for j in range(K):
+                    t = i * K + j
+                    if t < ON_TENSOR:
+                        nc.tensor.matmul(acc[:], identity[:], prod[:, j, :], start=(t == 0), stop=(t == ON_TENSOR - 1))
+            return acc, prod
 
-        def place(b, acc, pair, tap8):
+        def place(b, acc, prod):
             most = work.tile([P, N], F32, name="most")
-            nc.vector.tensor_tensor(most[:], acc[:], pair[:], ADD)
+            nc.vector.tensor_tensor(most[:], acc[:], prod[:, K - 2, :], ADD)
             window = all_windows[b]
-            nc.vector.tensor_tensor(window[:].indirect(offsets[:]), most[:], tap8, ADD)
+            nc.vector.tensor_tensor(window[:].indirect(offsets[:]), most[:], prod[:, K - 1, :], ADD)
             nc.sync.dma_start(out[b * P : (b + 1) * P, :], window[:])
 
         parts = multiply(0)
         for b in range(1, BLOCKS):
-            next_parts = multiply(b)
+            parts_ahead = multiply(b)
             place(b - 1, *parts)
-            parts = next_parts
+            parts = parts_ahead
         place(BLOCKS - 1, *parts)

@@ -24,12 +24,13 @@ def tile_locallyconnected2d_kernel(tc, base, x, wts, offs, out):
         tc.tile_pool(name="weights", bufs=BLOCKS) as weights,
         tc.tile_pool(name="work", bufs=2 * K) as work,
         tc.psum_pool(name="psum", bufs=2) as psum,
+        tc.psum_pool(name="psum_held", bufs=1) as psum_held,
     ):
         offsets = held.tile([P, N // 16], U16, name="offsets")
         nc.sync.dma_start(offsets[:], offs)
 
-        image = held.tile([P, N], F32, name="image")
-        nc.scalar.dma_start(image[:], x.rearrange("o h w -> (o h w)").partition_broadcast(P))
+        image_row = held.tile([1, N], F32, name="image_row")
+        nc.scalar.dma_start(image_row[:], x.rearrange("o h w -> o (h w)"))
 
         all_w, all_windows = [], []
         for b in range(BLOCKS + 1):
@@ -44,6 +45,11 @@ def tile_locallyconnected2d_kernel(tc, base, x, wts, offs, out):
 
         identity = held.tile([P, P], F32, name="identity")
         make_identity(nc, identity[:])
+
+        ones_row = held.tile([1, P], F32, name="ones_row")
+        nc.vector.memset(ones_row[:], 1.0)
+        image = psum_held.tile([P, N], F32, name="image")
+        nc.tensor.matmul(image[:], ones_row[:], image_row[:], start=True, stop=True)
 
         shifted = held.tile([P, K, (E + 2) * E], F32, name="shifted")
         nc.vector.memset(shifted[:], 0.0)

@@ -12,6 +12,7 @@ E, K = 16, 3
 N = E * E
 T = K * K
 BLOCKS = C // P
+AHEAD = 2
 ON_TENSOR = T - 2
 FLOPS = 2 * C * T * N
 
@@ -22,8 +23,8 @@ def tile_locallyconnected2d_kernel(tc, base, x, wts, offs, out):
         tc.tile_pool(name="held", bufs=1) as held,
         tc.tile_pool(name="windows", bufs=BLOCKS) as windows,
         tc.tile_pool(name="weights", bufs=BLOCKS) as weights,
-        tc.tile_pool(name="work", bufs=2 * K) as work,
-        tc.psum_pool(name="psum", bufs=2) as psum,
+        tc.tile_pool(name="work", bufs=(AHEAD + 1) * K) as work,
+        tc.psum_pool(name="psum", bufs=AHEAD + 1) as psum,
         tc.psum_pool(name="psum_held", bufs=1) as psum_held,
     ):
         offsets = held.tile([P, N // 16], U16, name="offsets")
@@ -33,14 +34,14 @@ def tile_locallyconnected2d_kernel(tc, base, x, wts, offs, out):
         nc.scalar.dma_start(image_row[:], x.rearrange("o h w -> o (h w)"))
 
         all_w, all_windows = [], []
-        for b in range(BLOCKS + 1):
+        for b in range(BLOCKS + AHEAD):
             if b < BLOCKS:
                 w = weights.tile([P, T, N], F32, name="w")
                 nc.sync.dma_start(w[:], wts[b * P : (b + 1) * P, :, :])
                 all_w.append(w)
-            if b > 0:
+            if b >= AHEAD:
                 window = windows.tile([P, S], F32, name="window")
-                nc.sync.dma_start(window[:], base[(b - 1) * P : b * P, :])
+                nc.sync.dma_start(window[:], base[(b - AHEAD) * P : (b - AHEAD + 1) * P, :])
                 all_windows.append(window)
 
         identity = held.tile([P, P], F32, name="identity")
@@ -82,9 +83,9 @@ def tile_locallyconnected2d_kernel(tc, base, x, wts, offs, out):
             nc.vector.tensor_tensor(window[:].indirect(offsets[:]), most[:], prod[:, K - 1, :], ADD)
             nc.sync.dma_start(out[b * P : (b + 1) * P, :], window[:])
 
-        parts = multiply(0)
-        for b in range(1, BLOCKS):
-            parts_ahead = multiply(b)
-            place(b - 1, *parts)
-            parts = parts_ahead
-        place(BLOCKS - 1, *parts)
+        parts = []
+        for b in range(BLOCKS + AHEAD):
+            if b < BLOCKS:
+                parts.append(multiply(b))
+            if b >= AHEAD:
+                place(b - AHEAD, *parts[b - AHEAD])

@@ -27,9 +27,6 @@ def tile_locallyconnected2d_kernel(tc, base, x, wts, offs, out):
         tc.psum_pool(name="psum", bufs=AHEAD + 1) as psum,
         tc.psum_pool(name="psum_held", bufs=1) as psum_held,
     ):
-        offsets = held.tile([P, N // 16], U16, name="offsets")
-        nc.sync.dma_start(offsets[:], offs)
-
         image_row = held.tile([1, N], F32, name="image_row")
         nc.scalar.dma_start(image_row[:], x.rearrange("o h w -> o (h w)"))
 
@@ -39,6 +36,9 @@ def tile_locallyconnected2d_kernel(tc, base, x, wts, offs, out):
                 w = weights.tile([P, T, N], F32, name="w")
                 nc.sync.dma_start(w[:], wts[b * P : (b + 1) * P, :, :])
                 all_w.append(w)
+            if b == AHEAD:
+                offsets = held.tile([P, N // 16], U16, name="offsets")
+                nc.sync.dma_start(offsets[:], offs)
             if b >= AHEAD:
                 window = windows.tile([P, S], F32, name="window")
                 nc.sync.dma_start(window[:], base[(b - AHEAD) * P : (b - AHEAD + 1) * P, :])

@@ -12,8 +12,10 @@ E, K = 16, 3
 N = E * E
 T = K * K
 BLOCKS = C // P
-AHEAD = 2
-ON_TENSOR = T - 2
+ROWS = BLOCKS * K
+LOADS = 3
+ROWS_PER_LOAD = ROWS // LOADS
+ON_TENSOR = T - K
 FLOPS = 2 * C * T * N
 
 
@@ -22,27 +24,28 @@ def tile_locallyconnected2d_kernel(tc, base, x, wts, offs, out):
     with (
         tc.tile_pool(name="held", bufs=1) as held,
         tc.tile_pool(name="windows", bufs=BLOCKS) as windows,
-        tc.tile_pool(name="weights", bufs=BLOCKS) as weights,
-        tc.tile_pool(name="work", bufs=(AHEAD + 1) * K) as work,
-        tc.psum_pool(name="psum", bufs=AHEAD + 1) as psum,
+        tc.tile_pool(name="weights", bufs=LOADS) as weights,
+        tc.tile_pool(name="work", bufs=ROWS) as work,
+        tc.psum_pool(name="psum", bufs=BLOCKS) as psum,
         tc.psum_pool(name="psum_held", bufs=1) as psum_held,
     ):
         image_row = held.tile([1, N], F32, name="image_row")
         nc.scalar.dma_start(image_row[:], x.rearrange("o h w -> o (h w)"))
 
+        wts_rows = wts.rearrange("(p k) (i j) n -> p (k i) j n", k=BLOCKS, j=K)
+        base_blocks = base.rearrange("(p k) s -> p k s", k=BLOCKS)
+        out_blocks = out.rearrange("(p k) s -> p k s", k=BLOCKS)
         all_w, all_windows = [], []
-        for b in range(BLOCKS + AHEAD):
-            if b < BLOCKS:
-                w = weights.tile([P, T, N], F32, name="w")
-                nc.sync.dma_start(w[:], wts[b * P : (b + 1) * P, :, :])
-                all_w.append(w)
-            if b == AHEAD:
-                offsets = held.tile([P, N // 16], U16, name="offsets")
-                nc.sync.dma_start(offsets[:], offs)
-            if b >= AHEAD:
-                window = windows.tile([P, S], F32, name="window")
-                nc.sync.dma_start(window[:], base[(b - AHEAD) * P : (b - AHEAD + 1) * P, :])
-                all_windows.append(window)
+        for l in range(LOADS):
+            w = weights.tile([P, ROWS_PER_LOAD, K, N], F32, name="w")
+            nc.sync.dma_start(w[:], wts_rows[:, l * ROWS_PER_LOAD : (l + 1) * ROWS_PER_LOAD, :, :])
+            all_w.append(w)
+        offsets = held.tile([P, N // 16], U16, name="offsets")
+        nc.sync.dma_start(offsets[:], offs)
+        for b in range(BLOCKS):
+            window = windows.tile([P, S], F32, name="window")
+            nc.sync.dma_start(window[:], base_blocks[:, b, :])
+            all_windows.append(window)
 
         identity = held.tile([P, P], F32, name="identity")
         make_identity(nc, identity[:])
@@ -66,26 +69,26 @@ def tile_locallyconnected2d_kernel(tc, base, x, wts, offs, out):
         def multiply(b):
             acc = psum.tile([P, N], F32, name="acc")
             for i in range(K):
+                load, row = divmod(b * K + i, ROWS_PER_LOAD)
                 prod = work.tile([P, K, N], F32, name="prod")
                 nc.vector.tensor_tensor(
-                    prod[:], all_w[b][:, i * K : (i + 1) * K, :], shifted[:, :, i * E : i * E + N], MULT
+                    prod[:], all_w[load][:, row, :, :], shifted[:, :, i * E : i * E + N], MULT
                 )
                 for j in range(K):
                     t = i * K + j
                     if t < ON_TENSOR:
                         nc.tensor.matmul(acc[:], identity[:], prod[:, j, :], start=(t == 0), stop=(t == ON_TENSOR - 1))
-            return acc, prod
+            taps_6_7 = work.tile([P, N], F32, name="taps_6_7")
+            nc.vector.tensor_tensor(taps_6_7[:], prod[:, 0, :], prod[:, 1, :], ADD)
+            return acc, taps_6_7, prod
 
-        def place(b, acc, prod):
+        def place(b, acc, taps_6_7, prod):
             most = work.tile([P, N], F32, name="most")
-            nc.vector.tensor_tensor(most[:], acc[:], prod[:, K - 2, :], ADD)
+            nc.vector.tensor_tensor(most[:], acc[:], taps_6_7[:], ADD)
             window = all_windows[b]
             nc.vector.tensor_tensor(window[:].indirect(offsets[:]), most[:], prod[:, K - 1, :], ADD)
-            nc.sync.dma_start(out[b * P : (b + 1) * P, :], window[:])
+            nc.sync.dma_start(out_blocks[:, b, :], window[:])
 
-        parts = []
-        for b in range(BLOCKS + AHEAD):
-            if b < BLOCKS:
-                parts.append(multiply(b))
-            if b >= AHEAD:
-                place(b - AHEAD, *parts[b - AHEAD])
+        parts = [multiply(b) for b in range(BLOCKS)]
+        for b in range(BLOCKS):
+            place(b, *parts[b])

@@ -30,7 +30,9 @@ def tile_locallyconnected2d_kernel(tc, base, x, wts, offs, out):
         tc.psum_pool(name="psum_held", bufs=1) as psum_held,
     ):
         image_row = held.tile([1, N], F32, name="image_row")
-        nc.scalar.dma_start(image_row[:], x.rearrange("o h w -> o (h w)"))
+        nc.sync.dma_start(image_row[:], x.rearrange("o h w -> o (h w)"))
+        offsets = held.tile([P, N // 16], U16, name="offsets")
+        nc.sync.dma_start(offsets[:], offs)
 
         wts_rows = wts.rearrange("(p k) (i j) n -> p (k i) j n", k=BLOCKS, j=K)
         base_blocks = base.rearrange("(p k) s -> p k s", k=BLOCKS)
@@ -38,13 +40,11 @@ def tile_locallyconnected2d_kernel(tc, base, x, wts, offs, out):
         all_w, all_windows = [], []
         for l in range(LOADS):
             w = weights.tile([P, ROWS_PER_LOAD, K, N], F32, name="w")
-            nc.sync.dma_start(w[:], wts_rows[:, l * ROWS_PER_LOAD : (l + 1) * ROWS_PER_LOAD, :, :])
+            nc.scalar.dma_start(w[:], wts_rows[:, l * ROWS_PER_LOAD : (l + 1) * ROWS_PER_LOAD, :, :])
             all_w.append(w)
-        offsets = held.tile([P, N // 16], U16, name="offsets")
-        nc.sync.dma_start(offsets[:], offs)
         for b in range(BLOCKS):
             window = windows.tile([P, S], F32, name="window")
-            nc.sync.dma_start(window[:], base_blocks[:, b, :])
+            nc.scalar.dma_start(window[:], base_blocks[:, b, :])
             all_windows.append(window)
 
         identity = held.tile([P, P], F32, name="identity")

@@ -12,9 +12,7 @@ E, K = 16, 3
 N = E * E
 T = K * K
 BLOCKS = C // P
-ROWS = BLOCKS * K
-LOADS = 3
-ROWS_PER_LOAD = ROWS // LOADS
+EDGE = E
 ON_TENSOR = T - K
 FLOPS = 2 * C * T * N
 
@@ -24,8 +22,8 @@ def tile_locallyconnected2d_kernel(tc, base, x, wts, offs, out):
     with (
         tc.tile_pool(name="held", bufs=1) as held,
         tc.tile_pool(name="windows", bufs=BLOCKS) as windows,
-        tc.tile_pool(name="weights", bufs=LOADS) as weights,
-        tc.tile_pool(name="work", bufs=ROWS) as work,
+        tc.tile_pool(name="weights", bufs=BLOCKS) as weights,
+        tc.tile_pool(name="work", bufs=BLOCKS * K) as work,
         tc.psum_pool(name="psum", bufs=BLOCKS) as psum,
         tc.psum_pool(name="psum_held", bufs=1) as psum_held,
     ):
@@ -34,13 +32,15 @@ def tile_locallyconnected2d_kernel(tc, base, x, wts, offs, out):
         offsets = held.tile([P, N // 16], U16, name="offsets")
         nc.sync.dma_start(offsets[:], offs)
 
-        wts_rows = wts.rearrange("(p k) (i j) n -> p (k i) j n", k=BLOCKS, j=K)
+        wts_runs = wts.rearrange("(p k) t n -> p k (t n)", k=BLOCKS)
         base_blocks = base.rearrange("(p k) s -> p k s", k=BLOCKS)
         out_blocks = out.rearrange("(p k) s -> p k s", k=BLOCKS)
         all_w, all_windows = [], []
-        for l in range(LOADS):
-            w = weights.tile([P, ROWS_PER_LOAD, K, N], F32, name="w")
-            nc.scalar.dma_start(w[:], wts_rows[:, l * ROWS_PER_LOAD : (l + 1) * ROWS_PER_LOAD, :, :])
+        for b in range(BLOCKS):
+            w = weights.tile([P, T * N], F32, name="w")
+            nc.gpsimd.memset(w[:, :EDGE], 0.0)
+            nc.gpsimd.memset(w[:, T * N - EDGE :], 0.0)
+            nc.scalar.dma_start(w[:, EDGE : T * N - EDGE], wts_runs[:, b, EDGE : T * N - EDGE])
             all_w.append(w)
         for b in range(BLOCKS):
             window = windows.tile([P, S], F32, name="window")
@@ -69,11 +69,9 @@ def tile_locallyconnected2d_kernel(tc, base, x, wts, offs, out):
         def multiply(b):
             acc = psum.tile([P, N], F32, name="acc")
             for i in range(K):
-                load, row = divmod(b * K + i, ROWS_PER_LOAD)
+                taps = all_w[b][:, i * K * N : (i + 1) * K * N].rearrange("p (j n) -> p j n", j=K)
                 prod = work.tile([P, K, N], F32, name="prod")
-                nc.vector.tensor_tensor(
-                    prod[:], all_w[load][:, row, :, :], shifted[:, :, i * E : i * E + N], MULT
-                )
+                nc.vector.tensor_tensor(prod[:], taps, shifted[:, :, i * E : i * E + N], MULT)
                 for j in range(K):
                     t = i * K + j
                     if t < ON_TENSOR:

@@ -14,6 +14,7 @@ T = K * K
 BLOCKS = C // P
 EDGE = E
 ON_TENSOR = T - K
+BURST = 256
 FLOPS = 2 * C * T * N
 
 
@@ -37,13 +38,13 @@ def tile_locallyconnected2d_kernel(tc, base, x, wts, offs, out):
         out_blocks = out.rearrange("(p k) s -> p k s", k=BLOCKS)
         all_w, all_windows = [], []
         for b in range(BLOCKS):
-            w = weights.tile([P, T * N], F32, name="w")
+            w = weights.tile([P, T * N], F32, name="w", align_bytes=BURST)
             nc.gpsimd.memset(w[:, :EDGE], 0.0)
             nc.gpsimd.memset(w[:, T * N - EDGE :], 0.0)
             nc.scalar.dma_start(w[:, EDGE : T * N - EDGE], wts_runs[:, b, EDGE : T * N - EDGE])
             all_w.append(w)
         for b in range(BLOCKS):
-            window = windows.tile([P, S], F32, name="window")
+            window = windows.tile([P, S], F32, name="window", align_bytes=BURST)
             nc.scalar.dma_start(window[:], base_blocks[:, b, :])
             all_windows.append(window)
 

@@ -12,8 +12,7 @@ E, K = 16, 3
 N = E * E
 T = K * K
 BLOCKS = C // P
-EDGE = E
-ON_TENSOR = T - K
+INNER = N - E
 BURST = 256
 FLOPS = 2 * C * T * N
 
@@ -24,7 +23,7 @@ def tile_locallyconnected2d_kernel(tc, base, x, wts, offs, out):
         tc.tile_pool(name="held", bufs=1) as held,
         tc.tile_pool(name="windows", bufs=BLOCKS) as windows,
         tc.tile_pool(name="weights", bufs=BLOCKS) as weights,
-        tc.tile_pool(name="work", bufs=BLOCKS * K) as work,
+        tc.tile_pool(name="work", bufs=2 * BLOCKS) as work,
         tc.psum_pool(name="psum", bufs=BLOCKS) as psum,
         tc.psum_pool(name="psum_held", bufs=1) as psum_held,
     ):
@@ -39,9 +38,7 @@ def tile_locallyconnected2d_kernel(tc, base, x, wts, offs, out):
         all_w, all_windows = [], []
         for b in range(BLOCKS):
             w = weights.tile([P, T * N], F32, name="w", align_bytes=BURST)
-            nc.gpsimd.memset(w[:, :EDGE], 0.0)
-            nc.gpsimd.memset(w[:, T * N - EDGE :], 0.0)
-            nc.scalar.dma_start(w[:, EDGE : T * N - EDGE], wts_runs[:, b, EDGE : T * N - EDGE])
+            nc.scalar.dma_start(w[:, E : T * N - E], wts_runs[:, b, E : T * N - E])
             all_w.append(w)
         for b in range(BLOCKS):
             window = windows.tile([P, S], F32, name="window", align_bytes=BURST)
@@ -56,36 +53,40 @@ def tile_locallyconnected2d_kernel(tc, base, x, wts, offs, out):
         image = psum_held.tile([P, N], F32, name="image")
         nc.tensor.matmul(image[:], ones_row[:], image_row[:], start=True, stop=True)
 
-        shifted = held.tile([P, K, (E + 2) * E], F32, name="shifted")
-        nc.vector.memset(shifted[:], 0.0)
-        shifted_rows = shifted[:].rearrange("p j (a q) -> p j a q", q=E)
-        image_rows = image[:].rearrange("p (h w) -> p h w", w=E)
+        shifted = held.tile([P, K, N], F32, name="shifted")
+        shifted_rows = shifted[:].rearrange("p j (h q) -> p j h q", q=E)
+        image_rows = image[:].rearrange("p (h q) -> p h q", q=E)
+        nc.vector.memset(shifted_rows[:, 0, :, 0:1], 0.0)
+        nc.vector.memset(shifted_rows[:, K - 1, :, E - 1 : E], 0.0)
         for j in range(K):
             first, last = max(0, 1 - j), min(E, E + 1 - j)
             nc.vector.tensor_copy(
-                shifted_rows[:, j, 1 : E + 1, first:last],
+                shifted_rows[:, j, :, first:last],
                 image_rows[:, :, first + j - 1 : last + j - 1],
             )
 
-        def multiply(b):
-            acc = psum.tile([P, N], F32, name="acc")
-            for i in range(K):
-                taps = all_w[b][:, i * K * N : (i + 1) * K * N].rearrange("p (j n) -> p j n", j=K)
-                prod = work.tile([P, K, N], F32, name="prod")
-                nc.vector.tensor_tensor(prod[:], taps, shifted[:, :, i * E : i * E + N], MULT)
-                for j in range(K):
-                    t = i * K + j
-                    if t < ON_TENSOR:
-                        nc.tensor.matmul(acc[:], identity[:], prod[:, j, :], start=(t == 0), stop=(t == ON_TENSOR - 1))
-            taps_6_7 = work.tile([P, N], F32, name="taps_6_7")
-            nc.vector.tensor_tensor(taps_6_7[:], prod[:, 0, :], prod[:, 1, :], ADD)
-            return acc, taps_6_7, prod
+        places = {0: slice(E, N), 2: slice(0, INNER)}
+        factors = {0: slice(0, INNER), 2: slice(E, N)}
 
-        def place(b, acc, taps_6_7, prod):
+        def multiply(b):
+            taps = all_w[b][:].rearrange("p (i j n) -> p i j n", i=K, j=K)
+            acc = psum.tile([P, N], F32, name="acc")
+            middle = work.tile([P, K, N], F32, name="middle")
+            nc.vector.tensor_tensor(middle[:], taps[:, 1, :, :], shifted[:], MULT)
+            nc.tensor.matmul(acc[:], identity[:], middle[:, 0, :], start=True, stop=False)
+            for i in (0, 2):
+                outer = work.tile([P, K, INNER], F32, name="outer")
+                nc.vector.tensor_tensor(outer[:], taps[:, i, :, places[i]], shifted[:, :, factors[i]], MULT)
+                for j in range(K):
+                    last_one = i == 2 and j == K - 1
+                    nc.tensor.matmul(acc[:, places[i]], identity[:], outer[:, j, :], start=False, stop=last_one)
+            return acc, middle
+
+        def place(b, acc, middle):
             most = work.tile([P, N], F32, name="most")
-            nc.vector.tensor_tensor(most[:], acc[:], taps_6_7[:], ADD)
+            nc.vector.tensor_tensor(most[:], acc[:], middle[:, 1, :], ADD)
             window = all_windows[b]
-            nc.vector.tensor_tensor(window[:].indirect(offsets[:]), most[:], prod[:, K - 1, :], ADD)
+            nc.vector.tensor_tensor(window[:].indirect(offsets[:]), most[:], middle[:, 2, :], ADD)
             nc.sync.dma_start(out_blocks[:, b, :], window[:])
 
         parts = [multiply(b) for b in range(BLOCKS)]

@@ -28,9 +28,7 @@ def tile_locallyconnected2d_kernel(tc, base, x, wts, offs, out):
         tc.psum_pool(name="psum_held", bufs=1) as psum_held,
     ):
         image_row = held.tile([1, N], F32, name="image_row")
-        nc.sync.dma_start(image_row[:], x.rearrange("o h w -> o (h w)"))
-        offsets = held.tile([P, N // 16], U16, name="offsets")
-        nc.sync.dma_start(offsets[:], offs)
+        nc.scalar.dma_start(image_row[:], x.rearrange("o h w -> o (h w)"))
 
         wts_runs = wts.rearrange("(p k) t n -> p k (t n)", k=BLOCKS)
         base_blocks = base.rearrange("(p k) s -> p k s", k=BLOCKS)
@@ -38,11 +36,13 @@ def tile_locallyconnected2d_kernel(tc, base, x, wts, offs, out):
         all_w, all_windows = [], []
         for b in range(BLOCKS):
             w = weights.tile([P, T * N], F32, name="w", align_bytes=BURST)
-            nc.scalar.dma_start(w[:, E : T * N - E], wts_runs[:, b, E : T * N - E])
+            nc.sync.dma_start(w[:, E : T * N - E], wts_runs[:, b, E : T * N - E])
             all_w.append(w)
+        offsets = held.tile([P, N // 16], U16, name="offsets")
+        nc.sync.dma_start(offsets[:], offs)
         for b in range(BLOCKS):
             window = windows.tile([P, S], F32, name="window", align_bytes=BURST)
-            nc.scalar.dma_start(window[:], base_blocks[:, b, :])
+            nc.sync.dma_start(window[:], base_blocks[:, b, :])
             all_windows.append(window)
 
         identity = held.tile([P, P], F32, name="identity")
@@ -87,7 +87,7 @@ def tile_locallyconnected2d_kernel(tc, base, x, wts, offs, out):
             nc.vector.tensor_tensor(most[:], acc[:], middle[:, 1, :], ADD)
             window = all_windows[b]
             nc.vector.tensor_tensor(window[:].indirect(offsets[:]), most[:], middle[:, 2, :], ADD)
-            nc.sync.dma_start(out_blocks[:, b, :], window[:])
+            nc.scalar.dma_start(out_blocks[:, b, :], window[:])
 
         parts = [multiply(b) for b in range(BLOCKS)]
         for b in range(BLOCKS):

@@ -12,6 +12,7 @@ E, K = 16, 3
 N = E * E
 T = K * K
 BLOCKS = C // P
+LOADS = ((0,), (1,), (2, 3))
 INNER = N - E
 BURST = 256
 FLOPS = 2 * C * T * N
@@ -22,7 +23,7 @@ def tile_locallyconnected2d_kernel(tc, base, x, wts, offs, out):
     with (
         tc.tile_pool(name="held", bufs=1) as held,
         tc.tile_pool(name="windows", bufs=BLOCKS) as windows,
-        tc.tile_pool(name="weights", bufs=BLOCKS) as weights,
+        tc.tile_pool(name="weights", bufs=1) as weights,
         tc.tile_pool(name="work", bufs=2 * BLOCKS) as work,
         tc.psum_pool(name="psum", bufs=BLOCKS) as psum,
         tc.psum_pool(name="psum_held", bufs=1) as psum_held,
@@ -30,14 +31,16 @@ def tile_locallyconnected2d_kernel(tc, base, x, wts, offs, out):
         image_row = held.tile([1, N], F32, name="image_row")
         nc.scalar.dma_start(image_row[:], x.rearrange("o h w -> o (h w)"))
 
-        wts_runs = wts.rearrange("(p k) t n -> p k (t n)", k=BLOCKS)
+        wts_runs = wts.rearrange("(p k) t n -> p (k t n)", k=BLOCKS)
+        run = T * N
         base_blocks = base.rearrange("(p k) s -> p k s", k=BLOCKS)
         out_blocks = out.rearrange("(p k) s -> p k s", k=BLOCKS)
         all_w, all_windows = [], []
-        for b in range(BLOCKS):
-            w = weights.tile([P, T * N], F32, name="w", align_bytes=BURST)
-            nc.sync.dma_start(w[:, E : T * N - E], wts_runs[:, b, E : T * N - E])
-            all_w.append(w)
+        for blocks in LOADS:
+            first, end = blocks[0] * run, (blocks[-1] + 1) * run
+            w = weights.tile([P, end - first], F32, name=f"w{blocks[0]}", align_bytes=BURST)
+            nc.sync.dma_start(w[:, E : end - first - E], wts_runs[:, first + E : end - E])
+            all_w += [w[:, k * run : (k + 1) * run] for k in range(len(blocks))]
         offsets = held.tile([P, N // 16], U16, name="offsets")
         nc.sync.dma_start(offsets[:], offs)
         for b in range(BLOCKS):
@@ -69,7 +72,7 @@ def tile_locallyconnected2d_kernel(tc, base, x, wts, offs, out):
         factors = {0: slice(0, INNER), 2: slice(E, N)}
 
         def multiply(b):
-            taps = all_w[b][:].rearrange("p (i j n) -> p i j n", i=K, j=K)
+            taps = all_w[b].rearrange("p (i j n) -> p i j n", i=K, j=K)
             acc = psum.tile([P, N], F32, name="acc")
             middle = work.tile([P, K, N], F32, name="middle")
             nc.vector.tensor_tensor(middle[:], taps[:, 1, :, :], shifted[:], MULT)

import concourse.mybir as mybir
from concourse.masks import make_identity

F32 = mybir.dt.float32
U16 = mybir.dt.uint16
MULT = mybir.AluOpType.mult
ADD = mybir.AluOpType.add

P = 128
C, S = 512, 2048
E, K = 16, 3
N = E * E
T = K * K
BLOCKS = C // P
LOADS = ((0,), (1,), (2, 3))
INNER = N - E
BURST = 256
FLOPS = 2 * C * T * N


def tile_locallyconnected2d_kernel(tc, base, x, wts, offs, out):
    nc = tc.nc
    with (
        tc.tile_pool(name="held", bufs=1) as held,
        tc.tile_pool(name="windows", bufs=BLOCKS) as windows,
        tc.tile_pool(name="weights", bufs=1) as weights,
        tc.tile_pool(name="work", bufs=2 * BLOCKS) as work,
        tc.psum_pool(name="psum", bufs=BLOCKS) as psum,
        tc.psum_pool(name="psum_held", bufs=1) as psum_held,
    ):
        image_row = held.tile([1, N], F32, name="image_row")
        nc.scalar.dma_start(image_row[:], x.rearrange("o h w -> o (h w)"))

        wts_runs = wts.rearrange("(p k) t n -> p (k t n)", k=BLOCKS)
        run = T * N
        base_blocks = base.rearrange("(p k) s -> p k s", k=BLOCKS)
        out_blocks = out.rearrange("(p k) s -> p k s", k=BLOCKS)
        all_w, all_windows = [], []
        for blocks in LOADS:
            first, end = blocks[0] * run, (blocks[-1] + 1) * run
            w = weights.tile([P, end - first], F32, name=f"w{blocks[0]}", align_bytes=BURST)
            nc.sync.dma_start(w[:, E : end - first - E], wts_runs[:, first + E : end - E])
            all_w += [w[:, k * run : (k + 1) * run] for k in range(len(blocks))]
        offsets = held.tile([P, N // 16], U16, name="offsets")
        nc.sync.dma_start(offsets[:], offs)
        for b in range(BLOCKS):
            window = windows.tile([P, S], F32, name="window", align_bytes=BURST)
            nc.sync.dma_start(window[:], base_blocks[:, b, :])
            all_windows.append(window)

        identity = held.tile([P, P], F32, name="identity")
        make_identity(nc, identity[:])

        ones_row = held.tile([1, P], F32, name="ones_row")
        nc.vector.memset(ones_row[:], 1.0)
        image = psum_held.tile([P, N], F32, name="image")
        nc.tensor.matmul(image[:], ones_row[:], image_row[:], start=True, stop=True)

        shifted = held.tile([P, K, N], F32, name="shifted")
        shifted_rows = shifted[:].rearrange("p j (h q) -> p j h q", q=E)
        image_rows = image[:].rearrange("p (h q) -> p h q", q=E)
        nc.vector.memset(shifted_rows[:, 0, :, 0:1], 0.0)
        nc.vector.memset(shifted_rows[:, K - 1, :, E - 1 : E], 0.0)
        for j in range(K):
            first, last = max(0, 1 - j), min(E, E + 1 - j)
            nc.vector.tensor_copy(
                shifted_rows[:, j, :, first:last],
                image_rows[:, :, first + j - 1 : last + j - 1],
            )

        places = {0: slice(E, N), 2: slice(0, INNER)}
        factors = {0: slice(0, INNER), 2: slice(E, N)}

        def multiply(b):
            taps = all_w[b].rearrange("p (i j n) -> p i j n", i=K, j=K)
            acc = psum.tile([P, N], F32, name="acc")
            middle = work.tile([P, K, N], F32, name="middle")
            nc.vector.tensor_tensor(middle[:], taps[:, 1, :, :], shifted[:], MULT)
            nc.tensor.matmul(acc[:], identity[:], middle[:, 0, :], start=True, stop=False)
            for i in (0, 2):
                outer = work.tile([P, K, INNER], F32, name="outer")
                nc.vector.tensor_tensor(outer[:], taps[:, i, :, places[i]], shifted[:, :, factors[i]], MULT)
                for j in range(K):
                    last_one = i == 2 and j == K - 1
                    nc.tensor.matmul(acc[:, places[i]], identity[:], outer[:, j, :], start=False, stop=last_one)
            return acc, middle

        def place(b, acc, middle):
            most = work.tile([P, N], F32, name="most")
            nc.vector.tensor_tensor(most[:], acc[:], middle[:, 1, :], ADD)
            window = all_windows[b]
            nc.vector.tensor_tensor(window[:].indirect(offsets[:]), most[:], middle[:, 2, :], ADD)
            nc.scalar.dma_start(out_blocks[:, b, :], window[:])

        parts = [multiply(b) for b in range(BLOCKS)]
        for b in range(BLOCKS):
            place(b, *parts[b])
